import numpy as np
import ml_dtypes


def mxq(x, axis, fmt="e4m3"):
    dtype, down = {"e4m3": (ml_dtypes.float8_e4m3fn, 7), "e5m2": (ml_dtypes.float8_e5m2, 14)}[fmt]
    v = np.moveaxis(np.asarray(x, np.float32).astype(ml_dtypes.bfloat16).astype(np.float64), axis, -1)
    blocks = v.reshape(v.shape[:-1] + (-1, 32))
    amax = np.abs(blocks).max(-1, keepdims=True)
    byte = np.maximum(np.where(amax > 0, np.frexp(amax)[1] - 1 + 127, 0) - down, 1)
    scale = np.exp2(byte - 127.0)
    codes = (blocks / scale).astype(np.float32).astype(dtype).astype(np.float64)
    return np.moveaxis((codes * scale).reshape(v.shape), -1, axis)


WIDE = False


def mx_kscale(k):
    if not WIDE:
        return np.ones(k)
    levels = np.array([10, -10, 5, -5, 0])
    if k % 512:
        return np.exp2(np.random.permutation(np.resize(levels, k // 32))).repeat(32)
    a = np.empty((k // 512, 16))
    for p in range(k // 512):
        a[p, :8] = np.random.permutation(np.resize(levels, 8))
        for g in range(8):
            far = levels[np.abs(levels - a[p, g]) >= 10]
            a[p, g + 8] = far[np.random.randint(len(far))]
    return np.exp2(a.ravel()).repeat(32)


BF16 = ml_dtypes.bfloat16


def bf(x):
    return np.asarray(x, np.float32).astype(BF16)


def f64(x):
    return np.asarray(x).astype(np.float64)


B, L, D, H, DK = 16, 256, 512, 4, 64
E = H * DK


def tropical_linear(t, w):
    return np.stack([np.max(t[n][:, None, :] + w[None, :, :], axis=-1) for n in range(t.shape[0])])


def split_heads(t):
    return t.reshape(B, L, H, DK).transpose(0, 2, 1, 3).reshape(B * H, L, DK)


def proj(xq, w, lam):
    return np.log1p(np.maximum(xq @ mxq(f64(w), 1, "e4m3").T, 0.0)) - lam


def setup_inputs():
    s = mx_kscale(D)
    return {"x": bf(np.random.standard_normal((B, L, D)) * s),
            "Wq": bf(np.random.standard_normal((E, D)) / np.sqrt(D) / s[None, :]),
            "Wk": bf(np.random.standard_normal((E, D)) / np.sqrt(D) / s[None, :]),
            "Wv": bf(np.random.standard_normal((E, D)) / np.sqrt(D) / s[None, :]),
            "lam": bf(1.0 + 0.1 * np.random.standard_normal((1, 1, E))),
            "Wq_trop": bf(np.random.standard_normal((DK, DK))),
            "Wk_trop": bf(np.random.standard_normal((DK, DK))),
            "Wv_trop": bf(np.random.standard_normal((DK, DK)))}


def reference(x, Wq, Wk, Wv, lam, Wq_trop, Wk_trop, Wv_trop):
    xq = mxq(f64(x), 2, "e4m3")
    lam = f64(lam)
    q = tropical_linear(split_heads(proj(xq, Wq, lam)), f64(Wq_trop))
    k = tropical_linear(split_heads(proj(xq, Wk, lam)), f64(Wk_trop))
    v = tropical_linear(split_heads(proj(xq, Wv, lam)), f64(Wv_trop))
    return q, k, v

@@ -1,0 +1,218 @@
+from contextlib import ExitStack
+
+import concourse.mybir as mybir
+from concourse.masks import make_identity
+
+F32 = mybir.dt.float32
+BF16 = mybir.dt.bfloat16
+U32 = mybir.dt.uint32
+U8 = mybir.dt.uint8
+FP8X4 = mybir.dt.float8_e4m3fn_x4
+ALU = mybir.AluOpType
+ACT = mybir.ActivationFunctionType
+AX = mybir.AxisListType
+
+P = 128
+B, L, D, H, DK = 16, 256, 512, 4, 64
+E = H * DK
+ROWS = B * L
+HALF = DK // 2
+CHUNK = 2048
+TILES = CHUNK // P
+PIECE = 512
+CLAMP = 128.0
+
+FLOPS = 2 * ROWS * D * 3 * E + 2 * 3 * ROWS * H * DK * DK
+
+
+def tile_tropicalattention_pa_t_kernel(
+    tc, x, Wq, Wk, Wv, lam, Wq_trop, Wk_trop, Wv_trop, out_0, out_1, out_2
+):
+    nc = tc.nc
+    weights = [Wq, Wk, Wv]
+    trops = [Wq_trop, Wk_trop, Wv_trop]
+    outs = [out_0, out_1, out_2]
+
+    with ExitStack() as ctx:
+        const = ctx.enter_context(tc.tile_pool(name="const", bufs=1))
+        keep = ctx.enter_context(tc.tile_pool(name="keep", bufs=1))
+        tmp = ctx.enter_context(tc.tile_pool(name="tmp", bufs=3))
+        psum = ctx.enter_context(tc.psum_pool(name="psum", bufs=8))
+
+        ident = const.tile([P, P], F32, name="ident")
+        make_identity(nc, ident[:])
+
+        x_codes = keep.tile([P, ROWS], U32, name="x_codes", align_bytes=64)
+        x_scales = keep.tile([P, ROWS], U8, name="x_scales", align_bytes=64)
+        w_codes = [keep.tile([P, 2 * P], U32, name="w_codes%d" % j, align_bytes=64) for j in range(3)]
+        w_scales = [keep.tile([P, 2 * P], U8, name="w_scales%d" % j, align_bytes=64) for j in range(3)]
+        diff = [keep.tile([P, ROWS], F32, name="diff%d" % j) for j in range(3)]
+        base = [keep.tile([P, ROWS], F32, name="base%d" % j) for j in range(3)]
+        delta = [keep.tile([P, DK], F32, name="delta%d" % j) for j in range(3)]
+        shift = [keep.tile([P, DK], F32, name="shift%d" % j) for j in range(3)]
+
+        with tc.tile_pool(name="stage", bufs=2) as stage, tc.tile_pool(name="small", bufs=1) as small:
+            w_sb = []
+            for j in range(3):
+                w_t = small.tile([P, 2 * D], BF16, name="w_sb%d" % j)
+                nc.sync.dma_start(
+                    out=w_t[:].rearrange("p (g k) -> p g k", g=2),
+                    in_=weights[j].rearrange("(g p) k -> p g k", p=P),
+                )
+                w_sb.append(w_t)
+            lam_b = small.tile([P, E], BF16, name="lam_b")
+            nc.scalar.dma_start(out=lam_b[:], in_=lam.rearrange("a b e -> (a b e)").partition_broadcast(P))
+            t_sb = []
+            for j in range(3):
+                t_t = small.tile([P, DK], BF16, name="t_sb%d" % j)
+                nc.scalar.dma_start(out=t_t[0:DK, :], in_=trops[j])
+                nc.scalar.dma_start(out=t_t[DK:P, :], in_=trops[j])
+                t_sb.append(t_t)
+
+            for j in range(3):
+                words = w_sb[j][:].bitcast(F32)
+                bank = psum.tile([P, 512], F32, name="bank", tag="bank")
+                for g in range(2):
+                    for u in range(2):
+                        nc.tensor.transpose(
+                            bank[:, u * 256 + g * P : u * 256 + (g + 1) * P],
+                            words[:, g * 256 + u : (g + 1) * 256 : 2],
+                            ident[:],
+                        )
+                gw = small.tile([P, 2 * D], BF16, name="gw%d" % j, align_bytes=64)
+                src = bank[:].rearrange("p (u h i l) -> p i h l u", u=2, h=H, i=2, l=HALF)
+                dst = gw[:].bitcast(F32).rearrange("p (i h l u) -> p i h l u", i=2, h=H, l=HALF, u=2)
+                for i in range(2):
+                    nc.vector.tensor_copy(out=dst[:, i], in_=src[:, i])
+                nc.vector.quantize_mx(out=w_codes[j][:].bitcast(FP8X4), scales=w_scales[j][:], in_=gw[:])
+
+            lam_v = lam_b[:].rearrange("p (h i l) -> p h i l", h=H, i=2, l=HALF)
+            for j in range(3):
+                xab = small.tile([P, 2 * P], F32, name="xab%d" % j)
+                for i in range(2):
+                    nc.vector.tensor_tensor(
+                        out=xab[:, i * P : (i + 1) * P].rearrange("p (h l) -> p h l", h=H),
+                        in0=t_sb[j][:, i * HALF : (i + 1) * HALF].unsqueeze(1).to_broadcast([P, H, HALF]),
+                        in1=lam_v[:, :, i, :],
+                        op=ALU.subtract,
+                    )
+                bank = psum.tile([P, 512], F32, name="bank", tag="bank")
+                for i in range(2):
+                    nc.tensor.transpose(bank[:, i * P : (i + 1) * P], xab[:, i * P : (i + 1) * P], ident[:])
+                tab = small.tile([P, 2, DK], F32, name="tab%d" % j)
+                nc.vector.tensor_copy(
+                    out=tab[:], in_=bank[:, 0 : 2 * P].rearrange("p (i o) -> p i o", i=2)[:, :, 0:DK]
+                )
+                nc.vector.tensor_tensor(out=delta[j][:], in0=tab[:, 0, :], in1=tab[:, 1, :], op=ALU.subtract)
+                nc.vector.tensor_scalar(
+                    out=delta[j][:], in0=delta[j][:], scalar1=CLAMP, scalar2=-CLAMP, op0=ALU.min, op1=ALU.max
+                )
+                nc.vector.scalar_tensor_tensor(
+                    out=shift[j][:], in0=tab[:, 0, :], scalar=-CLAMP, in1=tab[:, 1, :], op0=ALU.add, op1=ALU.max
+                )
+
+            x_view = x.flatten_outer_dims().rearrange("(t p) k -> p t k", p=P)
+            for c in range(4):
+                xs = stage.tile([P, 8 * D], BF16, name="xs", tag="xs")
+                nc.sync.dma_start(
+                    out=xs[:].rearrange("p (t k) -> p t k", t=8), in_=x_view[:, 8 * c : 8 * c + 8, :]
+                )
+                words = xs[:].bitcast(F32)
+                gx = stage.tile([P, 8 * D], BF16, name="gx", tag="gx", align_bytes=64)
+                gx_words = gx[:].bitcast(F32)
+                for pr in range(4):
+                    bank = psum.tile([P, 512], F32, name="bank", tag="bank")
+                    for tt in range(2):
+                        for u in range(2):
+                            t = 2 * pr + tt
+                            nc.tensor.transpose(
+                                bank[:, u * 256 + tt * P : u * 256 + (tt + 1) * P],
+                                words[:, t * 256 + u : (t + 1) * 256 : 2],
+                                ident[:],
+                            )
+                    dst = gx_words[:, pr * 512 : (pr + 1) * 512].rearrange("p (r u) -> p r u", u=2)
+                    src = bank[:].rearrange("p (u r) -> p r u", u=2)
+                    if pr % 2 == 0:
+                        nc.vector.tensor_copy(out=dst, in_=src)
+                    else:
+                        nc.scalar.copy(out=dst, in_=src)
+                nc.vector.quantize_mx(
+                    out=x_codes[:, c * 1024 : (c + 1) * 1024].bitcast(FP8X4),
+                    scales=x_scales[:, c * 1024 : (c + 1) * 1024],
+                    in_=gx[:],
+                )
+
+        relu_pool = ctx.enter_context(tc.tile_pool(name="relu_pool", bufs=3))
+        base_pool = ctx.enter_context(tc.tile_pool(name="base_pool", bufs=3))
+        y_pool = ctx.enter_context(tc.tile_pool(name="y_pool", bufs=2))
+
+        def prep_piece(j, c):
+            cols = slice(c * PIECE, (c + 1) * PIECE)
+            for i in range(2):
+                bank = psum.tile([P, 512], F32, name="bank", tag="bank")
+                nc.tensor.matmul_mx(
+                    out=bank[:],
+                    lhsT=w_codes[j][:, i * P : (i + 1) * P].bitcast(FP8X4),
+                    lhsT_scale=w_scales[j][:, i * P : (i + 1) * P],
+                    rhs=x_codes[:, cols].bitcast(FP8X4),
+                    rhs_scale=x_scales[:, cols],
+                    start=True,
+                    stop=True,
+                )
+                one_plus = tmp.tile([P, PIECE], F32, name="one_plus", tag="one_plus")
+                nc.vector.tensor_scalar(
+                    out=one_plus[:], in0=bank[:], scalar1=0.0, scalar2=1.0, op0=ALU.max, op1=ALU.add
+                )
+                target = diff[j] if i == 0 else base[j]
+                nc.scalar.activation(out=target[:, cols], in_=one_plus[:], func=ACT.Ln)
+            nc.vector.tensor_tensor(out=diff[j][:, cols], in0=diff[j][:, cols], in1=base[j][:, cols], op=ALU.subtract)
+
+        pieces = [(j, c) for j in range(3) for c in range(ROWS // PIECE)]
+        for k in range(4):
+            prep_piece(*pieces[k])
+        next_piece = 4
+
+        step = 0
+        for j in range(3):
+            for chunk in range(ROWS // CHUNK):
+                rows = slice(chunk * CHUNK, (chunk + 1) * CHUNK)
+                y = y_pool.tile([P, TILES, H, DK], F32, name="y", tag="y")
+                for o in range(DK):
+                    if step % 16 == 0 and next_piece < len(pieces):
+                        prep_piece(*pieces[next_piece])
+                        next_piece += 1
+                    step += 1
+                    gain = relu_pool.tile([P, CHUNK], F32, name="gain", tag="gain")
+                    nc.scalar.activation(
+                        out=gain[:], in_=diff[j][:, rows], func=ACT.Relu, bias=delta[j][:, o : o + 1], scale=1.0
+                    )
+                    floor = base_pool.tile([P, CHUNK], F32, name="floor", tag="floor")
+                    nc.gpsimd.tensor_scalar(
+                        out=floor[:], in0=base[j][:, rows], scalar1=shift[j][:, o : o + 1], scalar2=1.0,
+                        op0=ALU.add, op1=ALU.mult,
+                    )
+                    for q in range(TILES // 4):
+                        bank = psum.tile([P, 512], F32, name="bank", tag="bank")
+                        for s in range(4):
+                            t = 4 * q + s
+                            nc.tensor.matmul(
+                                out=bank[:, s * P : (s + 1) * P], lhsT=gain[:, t * P : (t + 1) * P], rhs=ident[:],
+                                is_transpose=True, start=True, stop=False,
+                            )
+                            nc.tensor.matmul(
+                                out=bank[:, s * P : (s + 1) * P], lhsT=floor[:, t * P : (t + 1) * P], rhs=ident[:],
+                                is_transpose=True, start=False, stop=True,
+                            )
+                        nc.vector.tensor_reduce(
+                            out=y[:, 4 * q : 4 * q + 4, :, o],
+                            in_=bank[:].rearrange("p (s h l) -> p s h l", s=4, h=H, l=HALF),
+                            axis=AX.X,
+                            op=ALU.max,
+                        )
+                for t in range(TILES):
+                    g = chunk * TILES + t
+                    b, l0 = g // 2, (g % 2) * P
+                    nc.sync.dma_start(
+                        out=outs[j][b * H : (b + 1) * H, l0 : l0 + P, :].rearrange("h p o -> p h o"),
+                        in_=y[:, t, :, :],
+                    )

@@ -21,6 +21,8 @@ CHUNK = 2048
 TILES = CHUNK // P
 PIECE = 512
 CLAMP = 128.0
+LOOK = 2
+SCALAR_FLOOR_EVERY = 12
 
 FLOPS = 2 * ROWS * D * 3 * E + 2 * 3 * ROWS * H * DK * DK
 
@@ -142,8 +144,8 @@ def tile_tropicalattention_pa_t_kernel(
                     in_=gx[:],
                 )
 
-        relu_pool = ctx.enter_context(tc.tile_pool(name="relu_pool", bufs=3))
-        base_pool = ctx.enter_context(tc.tile_pool(name="base_pool", bufs=3))
+        gain_pool = ctx.enter_context(tc.tile_pool(name="gain_pool", bufs=4))
+        floor_pool = ctx.enter_context(tc.tile_pool(name="floor_pool", bufs=4))
         y_pool = ctx.enter_context(tc.tile_pool(name="y_pool", bufs=2))
 
         def prep_piece(j, c):
@@ -167,48 +169,62 @@ def tile_tropicalattention_pa_t_kernel(
                 nc.scalar.activation(out=target[:, cols], in_=one_plus[:], func=ACT.Ln)
             nc.vector.tensor_tensor(out=diff[j][:, cols], in0=diff[j][:, cols], in1=base[j][:, cols], op=ALU.subtract)
 
+        units = [(j, chunk, o) for j in range(3) for chunk in range(ROWS // CHUNK) for o in range(DK)]
         pieces = [(j, c) for j in range(3) for c in range(ROWS // PIECE)]
+        made = {}
+
+        def produce(k):
+            j, chunk, o = units[k]
+            rows = slice(chunk * CHUNK, (chunk + 1) * CHUNK)
+            gain = gain_pool.tile([P, CHUNK], F32, name="gain", tag="gain")
+            nc.scalar.activation(
+                out=gain[:], in_=diff[j][:, rows], func=ACT.Relu, bias=delta[j][:, o : o + 1], scale=1.0
+            )
+            floor = floor_pool.tile([P, CHUNK], F32, name="floor", tag="floor")
+            if k % SCALAR_FLOOR_EVERY == SCALAR_FLOOR_EVERY - 1:
+                nc.scalar.activation(
+                    out=floor[:], in_=base[j][:, rows], func=ACT.Identity, bias=shift[j][:, o : o + 1], scale=1.0
+                )
+            else:
+                nc.gpsimd.tensor_scalar(
+                    out=floor[:], in0=base[j][:, rows], scalar1=shift[j][:, o : o + 1], scalar2=1.0,
+                    op0=ALU.add, op1=ALU.mult,
+                )
+            made[k] = [gain[:], floor[:]]
+
+        def consume(k, y):
+            o = units[k][2]
+            parts = made[k]
+            for q in range(TILES // 4):
+                bank = psum.tile([P, 512], F32, name="bank", tag="bank")
+                for s in range(4):
+                    t = 4 * q + s
+                    for n, part in enumerate(parts):
+                        nc.tensor.matmul(
+                            out=bank[:, s * P : (s + 1) * P], lhsT=part[:, t * P : (t + 1) * P], rhs=ident[:],
+                            is_transpose=True, start=(n == 0), stop=(n == len(parts) - 1),
+                        )
+                nc.vector.tensor_reduce(
+                    out=y[:, 4 * q : 4 * q + 4, :, o],
+                    in_=bank[:].rearrange("p (s h l) -> p s h l", s=4, h=H, l=HALF),
+                    axis=AX.X,
+                    op=ALU.max,
+                )
+
         for k in range(4):
             prep_piece(*pieces[k])
-        next_piece = 4
-
-        step = 0
-        for j in range(3):
-            for chunk in range(ROWS // CHUNK):
-                rows = slice(chunk * CHUNK, (chunk + 1) * CHUNK)
+        for k in range(LOOK):
+            produce(k)
+        for k in range(len(units)):
+            if k % 16 == 0 and 4 + k // 16 < len(pieces):
+                prep_piece(*pieces[4 + k // 16])
+            if k + LOOK < len(units):
+                produce(k + LOOK)
+            j, chunk, o = units[k]
+            if o == 0:
                 y = y_pool.tile([P, TILES, H, DK], F32, name="y", tag="y")
-                for o in range(DK):
-                    if step % 16 == 0 and next_piece < len(pieces):
-                        prep_piece(*pieces[next_piece])
-                        next_piece += 1
-                    step += 1
-                    gain = relu_pool.tile([P, CHUNK], F32, name="gain", tag="gain")
-                    nc.scalar.activation(
-                        out=gain[:], in_=diff[j][:, rows], func=ACT.Relu, bias=delta[j][:, o : o + 1], scale=1.0
-                    )
-                    floor = base_pool.tile([P, CHUNK], F32, name="floor", tag="floor")
-                    nc.gpsimd.tensor_scalar(
-                        out=floor[:], in0=base[j][:, rows], scalar1=shift[j][:, o : o + 1], scalar2=1.0,
-                        op0=ALU.add, op1=ALU.mult,
-                    )
-                    for q in range(TILES // 4):
-                        bank = psum.tile([P, 512], F32, name="bank", tag="bank")
-                        for s in range(4):
-                            t = 4 * q + s
-                            nc.tensor.matmul(
-                                out=bank[:, s * P : (s + 1) * P], lhsT=gain[:, t * P : (t + 1) * P], rhs=ident[:],
-                                is_transpose=True, start=True, stop=False,
-                            )
-                            nc.tensor.matmul(
-                                out=bank[:, s * P : (s + 1) * P], lhsT=floor[:, t * P : (t + 1) * P], rhs=ident[:],
-                                is_transpose=True, start=False, stop=True,
-                            )
-                        nc.vector.tensor_reduce(
-                            out=y[:, 4 * q : 4 * q + 4, :, o],
-                            in_=bank[:].rearrange("p (s h l) -> p s h l", s=4, h=H, l=HALF),
-                            axis=AX.X,
-                            op=ALU.max,
-                        )
+            consume(k, y)
+            if o == DK - 1:
                 for t in range(TILES):
                     g = chunk * TILES + t
                     b, l0 = g // 2, (g % 2) * P

@@ -148,7 +148,7 @@ def tile_tropicalattention_pa_t_kernel(
         floor_pool = ctx.enter_context(tc.tile_pool(name="floor_pool", bufs=4))
         y_pool = ctx.enter_context(tc.tile_pool(name="y_pool", bufs=2))
 
-        def prep_piece(j, c):
+        def prep_piece(j, c, subtracting):
             cols = slice(c * PIECE, (c + 1) * PIECE)
             for i in range(2):
                 bank = psum.tile([P, 512], F32, name="bank", tag="bank")
@@ -167,7 +167,7 @@ def tile_tropicalattention_pa_t_kernel(
                 )
                 target = diff[j] if i == 0 else base[j]
                 nc.scalar.activation(out=target[:, cols], in_=one_plus[:], func=ACT.Ln)
-            nc.vector.tensor_tensor(out=diff[j][:, cols], in0=diff[j][:, cols], in1=base[j][:, cols], op=ALU.subtract)
+            subtracting.tensor_tensor(out=diff[j][:, cols], in0=diff[j][:, cols], in1=base[j][:, cols], op=ALU.subtract)
 
         units = [(j, chunk, o) for j in range(3) for chunk in range(ROWS // CHUNK) for o in range(DK)]
         pieces = [(j, c) for j in range(3) for c in range(ROWS // PIECE)]
@@ -212,12 +212,12 @@ def tile_tropicalattention_pa_t_kernel(
                 )
 
         for k in range(4):
-            prep_piece(*pieces[k])
+            prep_piece(*pieces[k], nc.vector)
         for k in range(LOOK):
             produce(k)
         for k in range(len(units)):
             if k % 16 == 0 and 4 + k // 16 < len(pieces):
-                prep_piece(*pieces[4 + k // 16])
+                prep_piece(*pieces[4 + k // 16], nc.gpsimd)
             if k + LOOK < len(units):
                 produce(k + LOOK)
             j, chunk, o = units[k]

from contextlib import ExitStack

import concourse.mybir as mybir
from concourse.masks import make_identity

F32 = mybir.dt.float32
BF16 = mybir.dt.bfloat16
U32 = mybir.dt.uint32
U8 = mybir.dt.uint8
FP8X4 = mybir.dt.float8_e4m3fn_x4
ALU = mybir.AluOpType
ACT = mybir.ActivationFunctionType
AX = mybir.AxisListType

P = 128
B, L, D, H, DK = 16, 256, 512, 4, 64
E = H * DK
ROWS = B * L
HALF = DK // 2
CHUNK = 2048
TILES = CHUNK // P
PIECE = 512
CLAMP = 128.0
LOOK = 2
SCALAR_FLOOR_EVERY = 12

FLOPS = 2 * ROWS * D * 3 * E + 2 * 3 * ROWS * H * DK * DK


def tile_tropicalattention_pa_t_kernel(
    tc, x, Wq, Wk, Wv, lam, Wq_trop, Wk_trop, Wv_trop, out_0, out_1, out_2
):
    nc = tc.nc
    weights = [Wq, Wk, Wv]
    trops = [Wq_trop, Wk_trop, Wv_trop]
    outs = [out_0, out_1, out_2]

    with ExitStack() as ctx:
        const = ctx.enter_context(tc.tile_pool(name="const", bufs=1))
        keep = ctx.enter_context(tc.tile_pool(name="keep", bufs=1))
        tmp = ctx.enter_context(tc.tile_pool(name="tmp", bufs=3))
        psum = ctx.enter_context(tc.psum_pool(name="psum", bufs=8))

        ident = const.tile([P, P], F32, name="ident")
        make_identity(nc, ident[:])

        x_codes = keep.tile([P, ROWS], U32, name="x_codes", align_bytes=64)
        x_scales = keep.tile([P, ROWS], U8, name="x_scales", align_bytes=64)
        w_codes = [keep.tile([P, 2 * P], U32, name="w_codes%d" % j, align_bytes=64) for j in range(3)]
        w_scales = [keep.tile([P, 2 * P], U8, name="w_scales%d" % j, align_bytes=64) for j in range(3)]
        diff = [keep.tile([P, ROWS], F32, name="diff%d" % j) for j in range(3)]
        base = [keep.tile([P, ROWS], F32, name="base%d" % j) for j in range(3)]
        delta = [keep.tile([P, DK], F32, name="delta%d" % j) for j in range(3)]
        shift = [keep.tile([P, DK], F32, name="shift%d" % j) for j in range(3)]

        with tc.tile_pool(name="stage", bufs=2) as stage, tc.tile_pool(name="small", bufs=1) as small:
            w_sb = []
            for j in range(3):
                w_t = small.tile([P, 2 * D], BF16, name="w_sb%d" % j)
                nc.sync.dma_start(
                    out=w_t[:].rearrange("p (g k) -> p g k", g=2),
                    in_=weights[j].rearrange("(g p) k -> p g k", p=P),
                )
                w_sb.append(w_t)
            lam_b = small.tile([P, E], BF16, name="lam_b")
            nc.scalar.dma_start(out=lam_b[:], in_=lam.rearrange("a b e -> (a b e)").partition_broadcast(P))
            t_sb = []
            for j in range(3):
                t_t = small.tile([P, DK], BF16, name="t_sb%d" % j)
                nc.scalar.dma_start(out=t_t[0:DK, :], in_=trops[j])
                nc.scalar.dma_start(out=t_t[DK:P, :], in_=trops[j])
                t_sb.append(t_t)

            for j in range(3):
                words = w_sb[j][:].bitcast(F32)
                bank = psum.tile([P, 512], F32, name="bank", tag="bank")
                for g in range(2):
                    for u in range(2):
                        nc.tensor.transpose(
                            bank[:, u * 256 + g * P : u * 256 + (g + 1) * P],
                            words[:, g * 256 + u : (g + 1) * 256 : 2],
                            ident[:],
                        )
                gw = small.tile([P, 2 * D], BF16, name="gw%d" % j, align_bytes=64)
                src = bank[:].rearrange("p (u h i l) -> p i h l u", u=2, h=H, i=2, l=HALF)
                dst = gw[:].bitcast(F32).rearrange("p (i h l u) -> p i h l u", i=2, h=H, l=HALF, u=2)
                for i in range(2):
                    nc.vector.tensor_copy(out=dst[:, i], in_=src[:, i])
                nc.vector.quantize_mx(out=w_codes[j][:].bitcast(FP8X4), scales=w_scales[j][:], in_=gw[:])

            lam_v = lam_b[:].rearrange("p (h i l) -> p h i l", h=H, i=2, l=HALF)
            for j in range(3):
                xab = small.tile([P, 2 * P], F32, name="xab%d" % j)
                for i in range(2):
                    nc.vector.tensor_tensor(
                        out=xab[:, i * P : (i + 1) * P].rearrange("p (h l) -> p h l", h=H),
                        in0=t_sb[j][:, i * HALF : (i + 1) * HALF].unsqueeze(1).to_broadcast([P, H, HALF]),
                        in1=lam_v[:, :, i, :],
                        op=ALU.subtract,
                    )
                bank = psum.tile([P, 512], F32, name="bank", tag="bank")
                for i in range(2):
                    nc.tensor.transpose(bank[:, i * P : (i + 1) * P], xab[:, i * P : (i + 1) * P], ident[:])
                tab = small.tile([P, 2, DK], F32, name="tab%d" % j)
                nc.vector.tensor_copy(
                    out=tab[:], in_=bank[:, 0 : 2 * P].rearrange("p (i o) -> p i o", i=2)[:, :, 0:DK]
                )
                nc.vector.tensor_tensor(out=delta[j][:], in0=tab[:, 0, :], in1=tab[:, 1, :], op=ALU.subtract)
                nc.vector.tensor_scalar(
                    out=delta[j][:], in0=delta[j][:], scalar1=CLAMP, scalar2=-CLAMP, op0=ALU.min, op1=ALU.max
                )
                nc.vector.scalar_tensor_tensor(
                    out=shift[j][:], in0=tab[:, 0, :], scalar=-CLAMP, in1=tab[:, 1, :], op0=ALU.add, op1=ALU.max
                )

            x_view = x.flatten_outer_dims().rearrange("(t p) k -> p t k", p=P)
            for c in range(4):
                xs = stage.tile([P, 8 * D], BF16, name="xs", tag="xs")
                nc.sync.dma_start(
                    out=xs[:].rearrange("p (t k) -> p t k", t=8), in_=x_view[:, 8 * c : 8 * c + 8, :]
                )
                words = xs[:].bitcast(F32)
                gx = stage.tile([P, 8 * D], BF16, name="gx", tag="gx", align_bytes=64)
                gx_words = gx[:].bitcast(F32)
                for pr in range(4):
                    bank = psum.tile([P, 512], F32, name="bank", tag="bank")
                    for tt in range(2):
                        for u in range(2):
                            t = 2 * pr + tt
                            nc.tensor.transpose(
                                bank[:, u * 256 + tt * P : u * 256 + (tt + 1) * P],
                                words[:, t * 256 + u : (t + 1) * 256 : 2],
                                ident[:],
                            )
                    dst = gx_words[:, pr * 512 : (pr + 1) * 512].rearrange("p (r u) -> p r u", u=2)
                    src = bank[:].rearrange("p (u r) -> p r u", u=2)
                    if pr % 2 == 0:
                        nc.vector.tensor_copy(out=dst, in_=src)
                    else:
                        nc.scalar.copy(out=dst, in_=src)
                nc.vector.quantize_mx(
                    out=x_codes[:, c * 1024 : (c + 1) * 1024].bitcast(FP8X4),
                    scales=x_scales[:, c * 1024 : (c + 1) * 1024],
                    in_=gx[:],
                )

        gain_pool = ctx.enter_context(tc.tile_pool(name="gain_pool", bufs=4))
        floor_pool = ctx.enter_context(tc.tile_pool(name="floor_pool", bufs=4))
        y_pool = ctx.enter_context(tc.tile_pool(name="y_pool", bufs=2))

        def prep_piece(j, c, subtracting):
            cols = slice(c * PIECE, (c + 1) * PIECE)
            for i in range(2):
                bank = psum.tile([P, 512], F32, name="bank", tag="bank")
                nc.tensor.matmul_mx(
                    out=bank[:],
                    lhsT=w_codes[j][:, i * P : (i + 1) * P].bitcast(FP8X4),
                    lhsT_scale=w_scales[j][:, i * P : (i + 1) * P],
                    rhs=x_codes[:, cols].bitcast(FP8X4),
                    rhs_scale=x_scales[:, cols],
                    start=True,
                    stop=True,
                )
                one_plus = tmp.tile([P, PIECE], F32, name="one_plus", tag="one_plus")
                nc.vector.tensor_scalar(
                    out=one_plus[:], in0=bank[:], scalar1=0.0, scalar2=1.0, op0=ALU.max, op1=ALU.add
                )
                target = diff[j] if i == 0 else base[j]
                nc.scalar.activation(out=target[:, cols], in_=one_plus[:], func=ACT.Ln)
            subtracting.tensor_tensor(out=diff[j][:, cols], in0=diff[j][:, cols], in1=base[j][:, cols], op=ALU.subtract)

        units = [(j, chunk, o) for j in range(3) for chunk in range(ROWS // CHUNK) for o in range(DK)]
        pieces = [(j, c) for j in range(3) for c in range(ROWS // PIECE)]
        made = {}

        def produce(k):
            j, chunk, o = units[k]
            rows = slice(chunk * CHUNK, (chunk + 1) * CHUNK)
            gain = gain_pool.tile([P, CHUNK], F32, name="gain", tag="gain")
            nc.scalar.activation(
                out=gain[:], in_=diff[j][:, rows], func=ACT.Relu, bias=delta[j][:, o : o + 1], scale=1.0
            )
            floor = floor_pool.tile([P, CHUNK], F32, name="floor", tag="floor")
            if k % SCALAR_FLOOR_EVERY == SCALAR_FLOOR_EVERY - 1:
                nc.scalar.activation(
                    out=floor[:], in_=base[j][:, rows], func=ACT.Identity, bias=shift[j][:, o : o + 1], scale=1.0
                )
            else:
                nc.gpsimd.tensor_scalar(
                    out=floor[:], in0=base[j][:, rows], scalar1=shift[j][:, o : o + 1], scalar2=1.0,
                    op0=ALU.add, op1=ALU.mult,
                )
            made[k] = [gain[:], floor[:]]

        def consume(k, y):
            o = units[k][2]
            parts = made[k]
            for q in range(TILES // 4):
                bank = psum.tile([P, 512], F32, name="bank", tag="bank")
                for s in range(4):
                    t = 4 * q + s
                    for n, part in enumerate(parts):
                        nc.tensor.matmul(
                            out=bank[:, s * P : (s + 1) * P], lhsT=part[:, t * P : (t + 1) * P], rhs=ident[:],
                            is_transpose=True, start=(n == 0), stop=(n == len(parts) - 1),
                        )
                nc.vector.tensor_reduce(
                    out=y[:, 4 * q : 4 * q + 4, :, o],
                    in_=bank[:].rearrange("p (s h l) -> p s h l", s=4, h=H, l=HALF),
                    axis=AX.X,
                    op=ALU.max,
                )

        for k in range(4):
            prep_piece(*pieces[k], nc.vector)
        for k in range(LOOK):
            produce(k)
        for k in range(len(units)):
            if k % 16 == 0 and 4 + k // 16 < len(pieces):
                prep_piece(*pieces[4 + k // 16], nc.gpsimd)
            if k + LOOK < len(units):
                produce(k + LOOK)
            j, chunk, o = units[k]
            if o == 0:
                y = y_pool.tile([P, TILES, H, DK], F32, name="y", tag="y")
            consume(k, y)
            if o == DK - 1:
                for t in range(TILES):
                    g = chunk * TILES + t
                    b, l0 = g // 2, (g % 2) * P
                    nc.sync.dma_start(
                        out=outs[j][b * H : (b + 1) * H, l0 : l0 + P, :].rearrange("h p o -> p h o"),
                        in_=y[:, t, :, :],
                    )
